import numpy as np
import ml_dtypes


def mxq(x, axis, fmt="e4m3"):
    dtype, down = {"e4m3": (ml_dtypes.float8_e4m3fn, 7), "e5m2": (ml_dtypes.float8_e5m2, 14)}[fmt]
    v = np.moveaxis(np.asarray(x, np.float32).astype(ml_dtypes.bfloat16).astype(np.float64), axis, -1)
    blocks = v.reshape(v.shape[:-1] + (-1, 32))
    amax = np.abs(blocks).max(-1, keepdims=True)
    byte = np.maximum(np.where(amax > 0, np.frexp(amax)[1] - 1 + 127, 0) - down, 1)
    scale = np.exp2(byte - 127.0)
    codes = (blocks / scale).astype(np.float32).astype(dtype).astype(np.float64)
    return np.moveaxis((codes * scale).reshape(v.shape), -1, axis)


WIDE = False


def mx_kscale(k):
    if not WIDE:
        return np.ones(k)
    levels = np.array([10, -10, 5, -5, 0])
    if k % 512:
        return np.exp2(np.random.permutation(np.resize(levels, k // 32))).repeat(32)
    a = np.empty((k // 512, 16))
    for p in range(k // 512):
        a[p, :8] = np.random.permutation(np.resize(levels, 8))
        for g in range(8):
            far = levels[np.abs(levels - a[p, g]) >= 10]
            a[p, g + 8] = far[np.random.randint(len(far))]
    return np.exp2(a.ravel()).repeat(32)


BF16 = ml_dtypes.bfloat16


def bf(x):
    return np.asarray(x, np.float32).astype(BF16)


def f64(x):
    return np.asarray(x).astype(np.float64)


B, S, H, I = 2, 64, 512, 1024


def silu(v):
    return v / (1.0 + np.exp(-v))


def ternary(shape):
    return np.random.randint(-1, 2, shape).astype(np.float64)


def setup_inputs():
    s, t = mx_kscale(H), mx_kscale(I)
    x = np.random.standard_normal((B, S, H)) * s
    gate_w = ternary((I, H)) / s[None, :]
    up_w = ternary((I, H)) / s[None, :]
    down_w = ternary((H, I)) / t[None, :]
    gate_s = np.random.uniform(0.5, 2.5, I) / np.sqrt(H)
    up_s = np.random.uniform(0.5, 2.5, I) / np.sqrt(H) * t
    down_s = np.random.uniform(0.5, 2.5, H) / np.sqrt(I)
    return {"x": bf(x), "gate_w": bf(gate_w), "up_w": bf(up_w), "down_w": bf(down_w),
            "gate_s": bf(gate_s), "up_s": bf(up_s), "down_s": bf(down_s)}


def reference(x, gate_w, up_w, down_w, gate_s, up_s, down_s):
    x = f64(x)
    b, s, h = x.shape
    xq = mxq(x.reshape(b * s, h), 1, "e4m3")
    g = (xq @ mxq(f64(gate_w), 1, "e4m3").T) * f64(gate_s)
    u = (xq @ mxq(f64(up_w), 1, "e4m3").T) * f64(up_s)
    hdn = silu(g) * u
    out = (mxq(hdn, 1, "e4m3") @ mxq(f64(down_w), 1, "e4m3").T) * f64(down_s)
    return out.reshape(b, s, -1)

@@ -1,0 +1,225 @@
+from contextlib import ExitStack
+
+import concourse.mybir as mybir
+from concourse.masks import make_identity
+
+F32 = mybir.dt.float32
+BF16 = mybir.dt.bfloat16
+U32 = mybir.dt.uint32
+U8 = mybir.dt.uint8
+FP8X4 = mybir.dt.float8_e4m3fn_x4
+SILU = mybir.ActivationFunctionType.Silu
+MULT = mybir.AluOpType.mult
+
+P = 128
+PACK = 4
+K_PASS = P * PACK
+HIDDEN = 512
+INNER = 1024
+BANK = 512
+UNIT = 1024
+PAIRS = INNER // (2 * P)
+DOWN_UNITS = HIDDEN // P
+INNER_PASSES = INNER // K_PASS
+
+FLOPS = 2 * P * HIDDEN * INNER * 3
+
+
+def k_onto_partitions(nc, banks, identity, raw, grouped, copy_out):
+    words = raw[:].bitcast(F32)
+    blocks = words.shape[1] // P
+    bank = banks.tile([P, BANK], F32, tag="bank")
+    for b in range(blocks):
+        first = (b // 2) * 2 * P + b % 2
+        nc.tensor.transpose(bank[:, b * P : (b + 1) * P], words[:, first : first + 2 * P - b % 2 : 2], identity[:])
+    copy_out(
+        out=grouped[:].bitcast(F32).rearrange("p (s r v) -> p s r v", r=P, v=2),
+        in_=bank[:, 0 : blocks * P].rearrange("p (s v r) -> p s r v", v=2, r=P),
+    )
+
+
+def quantise(nc, grouped, codes, scales):
+    nc.vector.quantize_mx(out=codes[:].bitcast(FP8X4), scales=scales[:], in_=grouped[:])
+
+
+def tile_cudaternaryexpertmodule_s_kernel(
+    tc, x, gate_w, up_w, down_w, gate_s, up_s, down_s, out
+):
+    nc = tc.nc
+    x_rows = x.flatten_outer_dims()
+    out_rows = out.flatten_outer_dims()
+
+    gate_units = gate_w.rearrange("(c p h e) k -> c h p (e k)", p=P, h=2, e=2)
+    up_units = up_w.rearrange("(c p h e) k -> c h p (e k)", p=P, h=2, e=2)
+    down_units = down_w.rearrange("(j p) k -> j p k", p=P)
+    unit_views = []
+    for m in range(PAIRS):
+        unit_views.extend([gate_units[m // 2, m % 2], up_units[m // 2, m % 2]])
+    for j in range(DOWN_UNITS):
+        unit_views.append(down_units[j])
+    first_down = 2 * PAIRS
+
+    with ExitStack() as ctx:
+        ctx.enter_context(tc.manual_schedule())
+        fixed = ctx.enter_context(tc.tile_pool(name="fixed", bufs=1))
+        work = ctx.enter_context(tc.tile_pool(name="work", bufs=2))
+        banks = ctx.enter_context(tc.psum_pool(name="banks", bufs=8))
+
+        channel_rows = fixed.tile([P, 4 * P], BF16)
+        down_s_row = fixed.tile([P, HIDDEN], BF16)
+        ones = fixed.tile([P, P], BF16)
+        zero_column = fixed.tile([P, 1], F32)
+        nc.vector.memset(channel_rows[:], 0.0)
+        nc.vector.memset(down_s_row[:], 0.0)
+        nc.vector.memset(ones[:], 1.0)
+        nc.vector.memset(zero_column[:], 0.0)
+        identity = fixed.tile([P, P], F32)
+        make_identity(nc, identity[:])
+
+        channel_stage = fixed.tile([4, 4 * P], BF16)
+        down_s_stage = fixed.tile([1, HIDDEN], BF16)
+        nc.scalar.dma_start(out=channel_stage[0:2, :], in_=gate_s.rearrange("(r n) -> r n", r=2))
+        nc.scalar.dma_start(out=channel_stage[2:4, :], in_=up_s.rearrange("(r n) -> r n", r=2))
+        nc.scalar.dma_start(out=down_s_stage[:], in_=down_s.rearrange("(o n) -> o n", o=1))
+        x_raw = fixed.tile([P, HIDDEN], BF16)
+        nc.sync.dma_start(out=x_raw[:], in_=x_rows)
+        unit_raw = []
+        for n, view in enumerate(unit_views):
+            unit_raw.append(fixed.tile([P, UNIT], BF16, name="unit_raw%d" % n))
+            nc.sync.dma_start(out=unit_raw[n][:], in_=view)
+
+        table_warmer = fixed.tile([P, 1], F32)
+        nc.scalar.activation(out=table_warmer[:], in_=zero_column[:], func=SILU)
+
+        x_grouped = fixed.tile([P, P * PACK], BF16, align_bytes=64)
+        x_codes = fixed.tile([P, P], U32, align_bytes=64)
+        x_scales = fixed.tile([P, P], U8, align_bytes=64)
+        k_onto_partitions(nc, banks, identity, x_raw, x_grouped, nc.vector.tensor_copy)
+        quantise(nc, x_grouped, x_codes, x_scales)
+
+        nc.vector.tensor_copy(out=channel_rows[0:4, :], in_=channel_stage[:])
+        nc.vector.tensor_copy(out=down_s_row[0:1, :], in_=down_s_stage[:])
+
+        channel_scales = fixed.tile([P, 16], F32)
+        down_s_all = fixed.tile([P, HIDDEN], F32)
+
+        def spread_channel_scales():
+            channel_bank = banks.tile([P, BANK], F32, tag="bank")
+            channel_words = channel_rows[:].bitcast(F32)
+            for h in range(2):
+                nc.tensor.transpose(
+                    channel_bank[:, h * P : (h + 1) * P], channel_words[:, h : 2 * P - 1 + h : 2], identity[:]
+                )
+            nc.vector.tensor_copy(
+                out=channel_scales[:].rearrange("p (r h e) -> p h r e", h=2, e=2),
+                in_=channel_bank[:, 0 : 2 * P].bitcast(BF16).rearrange("p (h r e) -> p h r e", h=2, e=2)[:, :, 0:4, :],
+            )
+
+        def spread_down_s():
+            down_s_bank = banks.tile([P, BANK], F32, tag="bank")
+            nc.tensor.matmul(out=down_s_bank[:], lhsT=ones[:], rhs=down_s_row[:], start=True, stop=True)
+            nc.scalar.copy(out=down_s_all[:], in_=down_s_bank[:])
+
+        unit_grouped = []
+        unit_codes = []
+        unit_scales = []
+        hidden_rows = []
+        hidden_grouped = []
+        hidden_codes = []
+        hidden_scales = []
+
+        def transpose_unit(n):
+            unit_grouped.append(fixed.tile([P, UNIT], BF16, name="unit_grouped%d" % n, align_bytes=64))
+            k_onto_partitions(nc, banks, identity, unit_raw[n], unit_grouped[n], nc.scalar.copy)
+
+        def quantise_unit(n):
+            unit_codes.append(fixed.tile([P, UNIT // PACK], U32, name="unit_codes%d" % n, align_bytes=64))
+            unit_scales.append(fixed.tile([P, UNIT // PACK], U8, name="unit_scales%d" % n, align_bytes=64))
+            quantise(nc, unit_grouped[n], unit_codes[n], unit_scales[n])
+
+        def hidden_tiles(m):
+            g_bank = banks.tile([P, BANK], F32, tag="bank")
+            u_bank = banks.tile([P, BANK], F32, tag="bank")
+            for e in range(2):
+                cols = slice(e * P, (e + 1) * P)
+                for bank, n in ((g_bank, 2 * m), (u_bank, 2 * m + 1)):
+                    nc.tensor.matmul_mx(
+                        out=bank[:, cols],
+                        lhsT=unit_codes[n][:, cols].bitcast(FP8X4),
+                        lhsT_scale=unit_scales[n][:, cols],
+                        rhs=x_codes[:].bitcast(FP8X4),
+                        rhs_scale=x_scales[:],
+                        start=True,
+                        stop=True,
+                    )
+            if m % 2 == 0:
+                hidden_rows.append(fixed.tile([P, PACK * P], BF16, name="hidden_rows%d" % (m // 2)))
+            silu_g = work.tile([P, 2 * P], F32)
+            for e in range(2):
+                cols = slice(e * P, (e + 1) * P)
+                channel = 2 * m + e
+                t = channel % PACK
+                nc.scalar.activation(
+                    out=silu_g[:, cols],
+                    in_=g_bank[:, cols],
+                    func=SILU,
+                    scale=channel_scales[:, channel : channel + 1],
+                )
+                nc.vector.scalar_tensor_tensor(
+                    out=hidden_rows[m // 2][:, t * P : (t + 1) * P],
+                    in0=u_bank[:, cols],
+                    scalar=channel_scales[:, 8 + channel : 8 + channel + 1],
+                    in1=silu_g[:, cols],
+                    op0=MULT,
+                    op1=MULT,
+                )
+
+        def regroup_hidden(c):
+            hidden_grouped.append(fixed.tile([P, P * PACK], BF16, name="hidden_grouped%d" % c, align_bytes=64))
+            nc.vector.tensor_copy(
+                out=hidden_grouped[c][:].rearrange("p (w t) -> p w t", t=PACK),
+                in_=hidden_rows[c][:].rearrange("p (t w) -> p w t", t=PACK),
+            )
+
+        def quantise_hidden(c):
+            hidden_codes.append(fixed.tile([P, P], U32, name="hidden_codes%d" % c, align_bytes=64))
+            hidden_scales.append(fixed.tile([P, P], U8, name="hidden_scales%d" % c, align_bytes=64))
+            quantise(nc, hidden_grouped[c], hidden_codes[c], hidden_scales[c])
+
+        rounds = len(unit_views) // 2
+        for i in range(rounds):
+            transpose_unit(2 * i)
+            transpose_unit(2 * i + 1)
+            if i == 1:
+                spread_channel_scales()
+            if i == rounds - 1:
+                spread_down_s()
+            quantise_unit(2 * i)
+            if i >= 3 and i % 2 == 1:
+                quantise_hidden((i - 3) // 2)
+            quantise_unit(2 * i + 1)
+            m = i - 1
+            if 0 <= m < PAIRS:
+                hidden_tiles(m)
+                if m % 2 == 1:
+                    regroup_hidden(m // 2)
+
+        for j in range(DOWN_UNITS):
+            n = first_down + j
+            out_bank = banks.tile([P, BANK], F32, tag="bank")
+            for c in range(INNER_PASSES):
+                nc.tensor.matmul_mx(
+                    out=out_bank[:, 0:P],
+                    lhsT=hidden_codes[c][:].bitcast(FP8X4),
+                    lhsT_scale=hidden_scales[c][:],
+                    rhs=unit_codes[n][:, c * P : (c + 1) * P].bitcast(FP8X4),
+                    rhs_scale=unit_scales[n][:, c * P : (c + 1) * P],
+                    start=(c == 0),
+                    stop=(c == INNER_PASSES - 1),
+                )
+            channels = slice(j * P, (j + 1) * P)
+            result = work.tile([P, P], F32, bufs=DOWN_UNITS)
+            nc.vector.tensor_tensor(
+                out=result[:], in0=out_bank[:, 0:P], in1=down_s_all[:, channels], op=MULT
+            )
+            nc.sync.dma_start(out=out_rows[:, channels], in_=result[:])

@@ -9,6 +9,7 @@ U32 = mybir.dt.uint32
 U8 = mybir.dt.uint8
 FP8X4 = mybir.dt.float8_e4m3fn_x4
 SILU = mybir.ActivationFunctionType.Silu
+COPY = mybir.ActivationFunctionType.Copy
 MULT = mybir.AluOpType.mult
 
 P = 128
@@ -33,7 +34,7 @@ def k_onto_partitions(nc, banks, identity, raw, grouped, copy_out):
         first = (b // 2) * 2 * P + b % 2
         nc.tensor.transpose(bank[:, b * P : (b + 1) * P], words[:, first : first + 2 * P - b % 2 : 2], identity[:])
     copy_out(
-        out=grouped[:].bitcast(F32).rearrange("p (s r v) -> p s r v", r=P, v=2),
+        out=grouped.bitcast(F32).rearrange("p (s r v) -> p s r v", r=P, v=2),
         in_=bank[:, 0 : blocks * P].rearrange("p (s v r) -> p s r v", v=2, r=P),
     )
 
@@ -94,7 +95,7 @@ def tile_cudaternaryexpertmodule_s_kernel(
         x_grouped = fixed.tile([P, P * PACK], BF16, align_bytes=64)
         x_codes = fixed.tile([P, P], U32, align_bytes=64)
         x_scales = fixed.tile([P, P], U8, align_bytes=64)
-        k_onto_partitions(nc, banks, identity, x_raw, x_grouped, nc.vector.tensor_copy)
+        k_onto_partitions(nc, banks, identity, x_raw, x_grouped[:], nc.scalar.copy)
         quantise(nc, x_grouped, x_codes, x_scales)
 
         nc.vector.tensor_copy(out=channel_rows[0:4, :], in_=channel_stage[:])
@@ -118,67 +119,91 @@ def tile_cudaternaryexpertmodule_s_kernel(
         def spread_down_s():
             down_s_bank = banks.tile([P, BANK], F32, tag="bank")
             nc.tensor.matmul(out=down_s_bank[:], lhsT=ones[:], rhs=down_s_row[:], start=True, stop=True)
-            nc.scalar.copy(out=down_s_all[:], in_=down_s_bank[:])
+            nc.vector.tensor_copy(out=down_s_all[:], in_=down_s_bank[:])
 
-        unit_grouped = []
-        unit_codes = []
-        unit_scales = []
-        hidden_rows = []
+        codes = {}
+        scales = {}
+        grouped_of = {}
+        products = {}
         hidden_grouped = []
         hidden_codes = []
         hidden_scales = []
 
+        def open_units(first, count):
+            grouped = fixed.tile([P, count * UNIT], BF16, name="grouped%d" % first, align_bytes=64)
+            for n in range(count):
+                grouped_of[first + n] = grouped[:, n * UNIT : (n + 1) * UNIT]
+            return grouped
+
         def transpose_unit(n):
-            unit_grouped.append(fixed.tile([P, UNIT], BF16, name="unit_grouped%d" % n, align_bytes=64))
-            k_onto_partitions(nc, banks, identity, unit_raw[n], unit_grouped[n], nc.scalar.copy)
+            k_onto_partitions(nc, banks, identity, unit_raw[n], grouped_of[n], nc.scalar.copy)
 
-        def quantise_unit(n):
-            unit_codes.append(fixed.tile([P, UNIT // PACK], U32, name="unit_codes%d" % n, align_bytes=64))
-            unit_scales.append(fixed.tile([P, UNIT // PACK], U8, name="unit_scales%d" % n, align_bytes=64))
-            quantise(nc, unit_grouped[n], unit_codes[n], unit_scales[n])
+        def quantise_units(first, count, grouped):
+            width = UNIT // PACK
+            unit_codes = fixed.tile([P, count * width], U32, name="codes%d" % first, align_bytes=64)
+            unit_scales = fixed.tile([P, count * width], U8, name="scales%d" % first, align_bytes=64)
+            quantise(nc, grouped, unit_codes, unit_scales)
+            for n in range(count):
+                codes[first + n] = unit_codes[:, n * width : (n + 1) * width]
+                scales[first + n] = unit_scales[:, n * width : (n + 1) * width]
 
-        def hidden_tiles(m):
+        def multiply_gate_and_up(m):
             g_bank = banks.tile([P, BANK], F32, tag="bank")
             u_bank = banks.tile([P, BANK], F32, tag="bank")
+            products[m] = (g_bank, u_bank)
             for e in range(2):
                 cols = slice(e * P, (e + 1) * P)
                 for bank, n in ((g_bank, 2 * m), (u_bank, 2 * m + 1)):
                     nc.tensor.matmul_mx(
                         out=bank[:, cols],
-                        lhsT=unit_codes[n][:, cols].bitcast(FP8X4),
-                        lhsT_scale=unit_scales[n][:, cols],
+                        lhsT=codes[n][:, cols].bitcast(FP8X4),
+                        lhsT_scale=scales[n][:, cols],
                         rhs=x_codes[:].bitcast(FP8X4),
                         rhs_scale=x_scales[:],
                         start=True,
                         stop=True,
                     )
-            if m % 2 == 0:
-                hidden_rows.append(fixed.tile([P, PACK * P], BF16, name="hidden_rows%d" % (m // 2)))
-            silu_g = work.tile([P, 2 * P], F32)
-            for e in range(2):
-                cols = slice(e * P, (e + 1) * P)
-                channel = 2 * m + e
-                t = channel % PACK
-                nc.scalar.activation(
-                    out=silu_g[:, cols],
-                    in_=g_bank[:, cols],
-                    func=SILU,
-                    scale=channel_scales[:, channel : channel + 1],
-                )
-                nc.vector.scalar_tensor_tensor(
-                    out=hidden_rows[m // 2][:, t * P : (t + 1) * P],
-                    in0=u_bank[:, cols],
-                    scalar=channel_scales[:, 8 + channel : 8 + channel + 1],
-                    in1=silu_g[:, cols],
-                    op0=MULT,
-                    op1=MULT,
-                )
 
-        def regroup_hidden(c):
+        def hidden_tiles(c):
+            tiles = []
+            for t in range(PACK):
+                g_bank, u_bank = products[2 * c + t // 2]
+                cols = slice(t % 2 * P, (t % 2 + 1) * P)
+                column = PACK * c + t
+                gate_scale = channel_scales[:, column : column + 1]
+                up_scale = channel_scales[:, 8 + column : 9 + column]
+                tiles.append((g_bank[:, cols], u_bank[:, cols], gate_scale, up_scale))
+            return tiles
+
+        def hidden_grouped_tile(c):
             hidden_grouped.append(fixed.tile([P, P * PACK], BF16, name="hidden_grouped%d" % c, align_bytes=64))
+            return hidden_grouped[c][:].rearrange("p (w t) -> p w t", t=PACK)
+
+        def hidden_on_vector(c):
+            silu_g = fixed.tile([P, PACK * P], F32, name="silu_g%d" % c)
+            rows = fixed.tile([P, PACK * P], BF16, name="hidden_rows%d" % c)
+            for t, (g, u, gate_scale, up_scale) in enumerate(hidden_tiles(c)):
+                cols = slice(t * P, (t + 1) * P)
+                nc.scalar.activation(out=silu_g[:, cols], in_=g, func=SILU, scale=gate_scale)
+                nc.vector.scalar_tensor_tensor(
+                    out=rows[:, cols], in0=u, scalar=up_scale, in1=silu_g[:, cols], op0=MULT, op1=MULT
+                )
             nc.vector.tensor_copy(
-                out=hidden_grouped[c][:].rearrange("p (w t) -> p w t", t=PACK),
-                in_=hidden_rows[c][:].rearrange("p (t w) -> p w t", t=PACK),
+                out=hidden_grouped_tile(c), in_=rows[:].rearrange("p (t w) -> p w t", t=PACK)
+            )
+
+        def hidden_on_scalar(c):
+            silu_g = fixed.tile([P, PACK * P], F32, name="silu_g%d" % c)
+            scaled_u = fixed.tile([P, PACK * P], F32, name="scaled_u%d" % c)
+            for t, (g, u, gate_scale, up_scale) in enumerate(hidden_tiles(c)):
+                cols = slice(t * P, (t + 1) * P)
+                nc.scalar.activation(out=silu_g[:, cols], in_=g, func=SILU, scale=gate_scale)
+                nc.scalar.activation(out=scaled_u[:, cols], in_=u, func=COPY, scale=up_scale)
+            nc.vector.tensor_tensor(
+                out=hidden_grouped_tile(c),
+                in0=scaled_u[:].rearrange("p (t w) -> p w t", t=PACK),
+                in1=silu_g[:].rearrange("p (t w) -> p w t", t=PACK),
+                op=MULT,
             )
 
         def quantise_hidden(c):
@@ -186,40 +211,49 @@ def tile_cudaternaryexpertmodule_s_kernel(
             hidden_scales.append(fixed.tile([P, P], U8, name="hidden_scales%d" % c, align_bytes=64))
             quantise(nc, hidden_grouped[c], hidden_codes[c], hidden_scales[c])
 
-        rounds = len(unit_views) // 2
-        for i in range(rounds):
-            transpose_unit(2 * i)
-            transpose_unit(2 * i + 1)
-            if i == 1:
+        for n in range(first_down):
+            grouped = open_units(n, 1)
+            transpose_unit(n)
+            if n == 3:
                 spread_channel_scales()
-            if i == rounds - 1:
-                spread_down_s()
-            quantise_unit(2 * i)
-            if i >= 3 and i % 2 == 1:
-                quantise_hidden((i - 3) // 2)
-            quantise_unit(2 * i + 1)
-            m = i - 1
-            if 0 <= m < PAIRS:
-                hidden_tiles(m)
-                if m % 2 == 1:
-                    regroup_hidden(m // 2)
+            quantise_units(n, 1, grouped)
 
-        for j in range(DOWN_UNITS):
-            n = first_down + j
+        for m in range(PAIRS):
+            multiply_gate_and_up(m)
+        hidden_on_vector(0)
+        spread_down_s()
+        hidden_on_scalar(1)
+        quantise_hidden(0)
+        quantise_hidden(1)
+
+        first_pair = open_units(first_down, 2)
+        transpose_unit(first_down)
+        transpose_unit(first_down + 1)
+        last = [open_units(first_down + 2, 1), open_units(first_down + 3, 1)]
+        transpose_unit(first_down + 2)
+        transpose_unit(first_down + 3)
+        quantise_units(first_down, 2, first_pair)
+        quantise_units(first_down + 2, 1, last[0])
+        quantise_units(first_down + 3, 1, last[1])
+
+        for i in range(DOWN_UNITS // 2):
             out_bank = banks.tile([P, BANK], F32, tag="bank")
-            for c in range(INNER_PASSES):
-                nc.tensor.matmul_mx(
-                    out=out_bank[:, 0:P],
-                    lhsT=hidden_codes[c][:].bitcast(FP8X4),
-                    lhsT_scale=hidden_scales[c][:],
-                    rhs=unit_codes[n][:, c * P : (c + 1) * P].bitcast(FP8X4),
-                    rhs_scale=unit_scales[n][:, c * P : (c + 1) * P],
-                    start=(c == 0),
-                    stop=(c == INNER_PASSES - 1),
-                )
-            channels = slice(j * P, (j + 1) * P)
-            result = work.tile([P, P], F32, bufs=DOWN_UNITS)
+            for e in range(2):
+                n = first_down + 2 * i + e
+                for c in range(INNER_PASSES):
+                    cols = slice(c * P, (c + 1) * P)
+                    nc.tensor.matmul_mx(
+                        out=out_bank[:, e * P : (e + 1) * P],
+                        lhsT=hidden_codes[c][:].bitcast(FP8X4),
+                        lhsT_scale=hidden_scales[c][:],
+                        rhs=codes[n][:, cols].bitcast(FP8X4),
+                        rhs_scale=scales[n][:, cols],
+                        start=(c == 0),
+                        stop=(c == INNER_PASSES - 1),
+                    )
+            channels = slice(2 * i * P, 2 * (i + 1) * P)
+            result = work.tile([P, 2 * P], F32)
             nc.vector.tensor_tensor(
-                out=result[:], in0=out_bank[:, 0:P], in1=down_s_all[:, channels], op=MULT
+                out=result[:], in0=out_bank[:, 0 : 2 * P], in1=down_s_all[:, channels], op=MULT
             )
             nc.sync.dma_start(out=out_rows[:, channels], in_=result[:])

@@ -9,7 +9,6 @@ U32 = mybir.dt.uint32
 U8 = mybir.dt.uint8
 FP8X4 = mybir.dt.float8_e4m3fn_x4
 SILU = mybir.ActivationFunctionType.Silu
-COPY = mybir.ActivationFunctionType.Copy
 MULT = mybir.AluOpType.mult
 
 P = 128
@@ -27,7 +26,7 @@ FLOPS = 2 * P * HIDDEN * INNER * 3
 
 
 def k_onto_partitions(nc, banks, identity, raw, grouped, copy_out):
-    words = raw[:].bitcast(F32)
+    words = raw.bitcast(F32)
     blocks = words.shape[1] // P
     bank = banks.tile([P, BANK], F32, tag="bank")
     for b in range(blocks):
@@ -95,7 +94,7 @@ def tile_cudaternaryexpertmodule_s_kernel(
         x_grouped = fixed.tile([P, P * PACK], BF16, align_bytes=64)
         x_codes = fixed.tile([P, P], U32, align_bytes=64)
         x_scales = fixed.tile([P, P], U8, align_bytes=64)
-        k_onto_partitions(nc, banks, identity, x_raw, x_grouped[:], nc.scalar.copy)
+        k_onto_partitions(nc, banks, identity, x_raw[:], x_grouped[:], nc.scalar.copy)
         quantise(nc, x_grouped, x_codes, x_scales)
 
         nc.vector.tensor_copy(out=channel_rows[0:4, :], in_=channel_stage[:])
@@ -119,91 +118,75 @@ def tile_cudaternaryexpertmodule_s_kernel(
         def spread_down_s():
             down_s_bank = banks.tile([P, BANK], F32, tag="bank")
             nc.tensor.matmul(out=down_s_bank[:], lhsT=ones[:], rhs=down_s_row[:], start=True, stop=True)
-            nc.vector.tensor_copy(out=down_s_all[:], in_=down_s_bank[:])
+            nc.scalar.copy(out=down_s_all[:], in_=down_s_bank[:])
 
         codes = {}
         scales = {}
         grouped_of = {}
-        products = {}
+        hidden_rows = []
         hidden_grouped = []
         hidden_codes = []
         hidden_scales = []
 
-        def open_units(first, count):
-            grouped = fixed.tile([P, count * UNIT], BF16, name="grouped%d" % first, align_bytes=64)
-            for n in range(count):
-                grouped_of[first + n] = grouped[:, n * UNIT : (n + 1) * UNIT]
-            return grouped
+        def transpose(n, first=0, count=2):
+            grouped = fixed.tile([P, count * K_PASS], BF16, name="grouped%d_%d" % (n, first), align_bytes=64)
+            raw = unit_raw[n][:, first * K_PASS : (first + count) * K_PASS]
+            k_onto_partitions(nc, banks, identity, raw, grouped[:], nc.scalar.copy)
+            grouped_of[n, first] = grouped
 
-        def transpose_unit(n):
-            k_onto_partitions(nc, banks, identity, unit_raw[n], grouped_of[n], nc.scalar.copy)
+        def quantise_tiles(n, first=0, count=2):
+            unit_codes = fixed.tile([P, count * P], U32, name="codes%d_%d" % (n, first), align_bytes=64)
+            unit_scales = fixed.tile([P, count * P], U8, name="scales%d_%d" % (n, first), align_bytes=64)
+            quantise(nc, grouped_of[n, first], unit_codes, unit_scales)
+            for i in range(count):
+                cols = slice(i * P, (i + 1) * P)
+                codes[n, first + i] = unit_codes[:, cols].bitcast(FP8X4)
+                scales[n, first + i] = unit_scales[:, cols]
 
-        def quantise_units(first, count, grouped):
-            width = UNIT // PACK
-            unit_codes = fixed.tile([P, count * width], U32, name="codes%d" % first, align_bytes=64)
-            unit_scales = fixed.tile([P, count * width], U8, name="scales%d" % first, align_bytes=64)
-            quantise(nc, grouped, unit_codes, unit_scales)
-            for n in range(count):
-                codes[first + n] = unit_codes[:, n * width : (n + 1) * width]
-                scales[first + n] = unit_scales[:, n * width : (n + 1) * width]
+        def multiply(n, bank):
+            for e in range(2):
+                nc.tensor.matmul_mx(
+                    out=bank[:, e * P : (e + 1) * P],
+                    lhsT=codes[n, e],
+                    lhsT_scale=scales[n, e],
+                    rhs=x_codes[:].bitcast(FP8X4),
+                    rhs_scale=x_scales[:],
+                    start=True,
+                    stop=True,
+                )
 
-        def multiply_gate_and_up(m):
+        def hidden_tiles(m):
             g_bank = banks.tile([P, BANK], F32, tag="bank")
             u_bank = banks.tile([P, BANK], F32, tag="bank")
-            products[m] = (g_bank, u_bank)
+            multiply(2 * m, g_bank)
+            multiply(2 * m + 1, u_bank)
+            if m % 2 == 0:
+                hidden_rows.append(fixed.tile([P, PACK * P], BF16, name="hidden_rows%d" % (m // 2)))
+            silu_g = work.tile([P, 2 * P], F32)
             for e in range(2):
                 cols = slice(e * P, (e + 1) * P)
-                for bank, n in ((g_bank, 2 * m), (u_bank, 2 * m + 1)):
-                    nc.tensor.matmul_mx(
-                        out=bank[:, cols],
-                        lhsT=codes[n][:, cols].bitcast(FP8X4),
-                        lhsT_scale=scales[n][:, cols],
-                        rhs=x_codes[:].bitcast(FP8X4),
-                        rhs_scale=x_scales[:],
-                        start=True,
-                        stop=True,
-                    )
-
-        def hidden_tiles(c):
-            tiles = []
-            for t in range(PACK):
-                g_bank, u_bank = products[2 * c + t // 2]
-                cols = slice(t % 2 * P, (t % 2 + 1) * P)
-                column = PACK * c + t
-                gate_scale = channel_scales[:, column : column + 1]
-                up_scale = channel_scales[:, 8 + column : 9 + column]
-                tiles.append((g_bank[:, cols], u_bank[:, cols], gate_scale, up_scale))
-            return tiles
-
-        def hidden_grouped_tile(c):
-            hidden_grouped.append(fixed.tile([P, P * PACK], BF16, name="hidden_grouped%d" % c, align_bytes=64))
-            return hidden_grouped[c][:].rearrange("p (w t) -> p w t", t=PACK)
-
-        def hidden_on_vector(c):
-            silu_g = fixed.tile([P, PACK * P], F32, name="silu_g%d" % c)
-            rows = fixed.tile([P, PACK * P], BF16, name="hidden_rows%d" % c)
-            for t, (g, u, gate_scale, up_scale) in enumerate(hidden_tiles(c)):
-                cols = slice(t * P, (t + 1) * P)
-                nc.scalar.activation(out=silu_g[:, cols], in_=g, func=SILU, scale=gate_scale)
-                nc.vector.scalar_tensor_tensor(
-                    out=rows[:, cols], in0=u, scalar=up_scale, in1=silu_g[:, cols], op0=MULT, op1=MULT
+                channel = 2 * m + e
+                t = channel % PACK
+                nc.scalar.activation(
+                    out=silu_g[:, cols],
+                    in_=g_bank[:, cols],
+                    func=SILU,
+                    scale=channel_scales[:, channel : channel + 1],
                 )
-            nc.vector.tensor_copy(
-                out=hidden_grouped_tile(c), in_=rows[:].rearrange("p (t w) -> p w t", t=PACK)
-            )
+                nc.vector.scalar_tensor_tensor(
+                    out=hidden_rows[m // 2][:, t * P : (t + 1) * P],
+                    in0=u_bank[:, cols],
+                    scalar=channel_scales[:, 8 + channel : 9 + channel],
+                    in1=silu_g[:, cols],
+                    op0=MULT,
+                    op1=MULT,
+                )
 
-        def hidden_on_scalar(c):
-            silu_g = fixed.tile([P, PACK * P], F32, name="silu_g%d" % c)
-            scaled_u = fixed.tile([P, PACK * P], F32, name="scaled_u%d" % c)
-            for t, (g, u, gate_scale, up_scale) in enumerate(hidden_tiles(c)):
-                cols = slice(t * P, (t + 1) * P)
-                nc.scalar.activation(out=silu_g[:, cols], in_=g, func=SILU, scale=gate_scale)
-                nc.scalar.activation(out=scaled_u[:, cols], in_=u, func=COPY, scale=up_scale)
-            nc.vector.tensor_tensor(
-                out=hidden_grouped_tile(c),
-                in0=scaled_u[:].rearrange("p (t w) -> p w t", t=PACK),
-                in1=silu_g[:].rearrange("p (t w) -> p w t", t=PACK),
-                op=MULT,
+        def regroup_hidden(c):
+            hidden_grouped.append(fixed.tile([P, P * PACK], BF16, name="hidden_grouped%d" % c, align_bytes=64))
+            nc.vector.tensor_copy(
+                out=hidden_grouped[c][:].rearrange("p (w t) -> p w t", t=PACK),
+                in_=hidden_rows[c][:].rearrange("p (t w) -> p w t", t=PACK),
             )
 
         def quantise_hidden(c):
@@ -211,49 +194,51 @@ def tile_cudaternaryexpertmodule_s_kernel(
             hidden_scales.append(fixed.tile([P, P], U8, name="hidden_scales%d" % c, align_bytes=64))
             quantise(nc, hidden_grouped[c], hidden_codes[c], hidden_scales[c])
 
-        for n in range(first_down):
-            grouped = open_units(n, 1)
-            transpose_unit(n)
-            if n == 3:
+        for n in range(6):
+            transpose(n)
+            if n == 1:
                 spread_channel_scales()
-            quantise_units(n, 1, grouped)
-
-        for m in range(PAIRS):
-            multiply_gate_and_up(m)
-        hidden_on_vector(0)
-        spread_down_s()
-        hidden_on_scalar(1)
+            quantise_tiles(n)
+        hidden_tiles(0)
+        for n in (6, 7):
+            transpose(n)
+            quantise_tiles(n)
+        transpose(8)
+        hidden_tiles(1)
+        quantise_tiles(8)
+        regroup_hidden(0)
+        transpose(9)
+        hidden_tiles(2)
+        hidden_tiles(3)
         quantise_hidden(0)
+        regroup_hidden(1)
+        quantise_tiles(9)
         quantise_hidden(1)
+        transpose(10)
+        quantise_tiles(10)
+        for c in range(INNER_PASSES):
+            transpose(11, c, 1)
+        spread_down_s()
+        for c in range(INNER_PASSES):
+            quantise_tiles(11, c, 1)
 
-        first_pair = open_units(first_down, 2)
-        transpose_unit(first_down)
-        transpose_unit(first_down + 1)
-        last = [open_units(first_down + 2, 1), open_units(first_down + 3, 1)]
-        transpose_unit(first_down + 2)
-        transpose_unit(first_down + 3)
-        quantise_units(first_down, 2, first_pair)
-        quantise_units(first_down + 2, 1, last[0])
-        quantise_units(first_down + 3, 1, last[1])
-
-        for i in range(DOWN_UNITS // 2):
+        for blocks in ((0, 1), (2,), (3,)):
             out_bank = banks.tile([P, BANK], F32, tag="bank")
-            for e in range(2):
-                n = first_down + 2 * i + e
+            width = len(blocks) * P
+            for b, j in enumerate(blocks):
                 for c in range(INNER_PASSES):
-                    cols = slice(c * P, (c + 1) * P)
                     nc.tensor.matmul_mx(
-                        out=out_bank[:, e * P : (e + 1) * P],
+                        out=out_bank[:, b * P : (b + 1) * P],
                         lhsT=hidden_codes[c][:].bitcast(FP8X4),
                         lhsT_scale=hidden_scales[c][:],
-                        rhs=codes[n][:, cols].bitcast(FP8X4),
-                        rhs_scale=scales[n][:, cols],
+                        rhs=codes[first_down + j, c],
+                        rhs_scale=scales[first_down + j, c],
                         start=(c == 0),
                         stop=(c == INNER_PASSES - 1),
                     )
-            channels = slice(2 * i * P, 2 * (i + 1) * P)
-            result = work.tile([P, 2 * P], F32)
+            channels = slice(blocks[0] * P, blocks[0] * P + width)
+            result = work.tile([P, 2 * P], F32, bufs=3)
             nc.vector.tensor_tensor(
-                out=result[:], in0=out_bank[:, 0 : 2 * P], in1=down_s_all[:, channels], op=MULT
+                out=result[:, 0:width], in0=out_bank[:, 0:width], in1=down_s_all[:, channels], op=MULT
             )
-            nc.sync.dma_start(out=out_rows[:, channels], in_=result[:])
+            nc.sync.dma_start(out=out_rows[:, channels], in_=result[:, 0:width])

from contextlib import ExitStack

import concourse.mybir as mybir
from concourse.masks import make_identity

F32 = mybir.dt.float32
BF16 = mybir.dt.bfloat16
U32 = mybir.dt.uint32
U8 = mybir.dt.uint8
FP8X4 = mybir.dt.float8_e4m3fn_x4
SILU = mybir.ActivationFunctionType.Silu
MULT = mybir.AluOpType.mult

P = 128
PACK = 4
K_PASS = P * PACK
HIDDEN = 512
INNER = 1024
BANK = 512
UNIT = 1024
PAIRS = INNER // (2 * P)
DOWN_UNITS = HIDDEN // P
INNER_PASSES = INNER // K_PASS

FLOPS = 2 * P * HIDDEN * INNER * 3


def k_onto_partitions(nc, banks, identity, raw, grouped, copy_out):
    words = raw.bitcast(F32)
    blocks = words.shape[1] // P
    bank = banks.tile([P, BANK], F32, tag="bank")
    for b in range(blocks):
        first = (b // 2) * 2 * P + b % 2
        nc.tensor.transpose(bank[:, b * P : (b + 1) * P], words[:, first : first + 2 * P - b % 2 : 2], identity[:])
    copy_out(
        out=grouped.bitcast(F32).rearrange("p (s r v) -> p s r v", r=P, v=2),
        in_=bank[:, 0 : blocks * P].rearrange("p (s v r) -> p s r v", v=2, r=P),
    )


def quantise(nc, grouped, codes, scales):
    nc.vector.quantize_mx(out=codes[:].bitcast(FP8X4), scales=scales[:], in_=grouped[:])


def tile_cudaternaryexpertmodule_s_kernel(
    tc, x, gate_w, up_w, down_w, gate_s, up_s, down_s, out
):
    nc = tc.nc
    x_rows = x.flatten_outer_dims()
    out_rows = out.flatten_outer_dims()

    gate_units = gate_w.rearrange("(c p h e) k -> c h p (e k)", p=P, h=2, e=2)
    up_units = up_w.rearrange("(c p h e) k -> c h p (e k)", p=P, h=2, e=2)
    down_units = down_w.rearrange("(j p) k -> j p k", p=P)
    unit_views = []
    for m in range(PAIRS):
        unit_views.extend([gate_units[m // 2, m % 2], up_units[m // 2, m % 2]])
    for j in range(DOWN_UNITS):
        unit_views.append(down_units[j])
    first_down = 2 * PAIRS

    with ExitStack() as ctx:
        ctx.enter_context(tc.manual_schedule())
        fixed = ctx.enter_context(tc.tile_pool(name="fixed", bufs=1))
        work = ctx.enter_context(tc.tile_pool(name="work", bufs=2))
        banks = ctx.enter_context(tc.psum_pool(name="banks", bufs=8))

        channel_rows = fixed.tile([P, 4 * P], BF16)
        down_s_row = fixed.tile([P, HIDDEN], BF16)
        ones = fixed.tile([P, P], BF16)
        zero_column = fixed.tile([P, 1], F32)
        nc.vector.memset(channel_rows[:], 0.0)
        nc.vector.memset(down_s_row[:], 0.0)
        nc.vector.memset(ones[:], 1.0)
        nc.vector.memset(zero_column[:], 0.0)
        identity = fixed.tile([P, P], F32)
        make_identity(nc, identity[:])

        channel_stage = fixed.tile([4, 4 * P], BF16)
        down_s_stage = fixed.tile([1, HIDDEN], BF16)
        nc.scalar.dma_start(out=channel_stage[0:2, :], in_=gate_s.rearrange("(r n) -> r n", r=2))
        nc.scalar.dma_start(out=channel_stage[2:4, :], in_=up_s.rearrange("(r n) -> r n", r=2))
        nc.scalar.dma_start(out=down_s_stage[:], in_=down_s.rearrange("(o n) -> o n", o=1))
        x_raw = fixed.tile([P, HIDDEN], BF16)
        nc.sync.dma_start(out=x_raw[:], in_=x_rows)
        unit_raw = []
        for n, view in enumerate(unit_views):
            unit_raw.append(fixed.tile([P, UNIT], BF16, name="unit_raw%d" % n))
            nc.sync.dma_start(out=unit_raw[n][:], in_=view)

        table_warmer = fixed.tile([P, 1], F32)
        nc.scalar.activation(out=table_warmer[:], in_=zero_column[:], func=SILU)

        x_grouped = fixed.tile([P, P * PACK], BF16, align_bytes=64)
        x_codes = fixed.tile([P, P], U32, align_bytes=64)
        x_scales = fixed.tile([P, P], U8, align_bytes=64)
        k_onto_partitions(nc, banks, identity, x_raw[:], x_grouped[:], nc.scalar.copy)
        quantise(nc, x_grouped, x_codes, x_scales)

        nc.vector.tensor_copy(out=channel_rows[0:4, :], in_=channel_stage[:])
        nc.vector.tensor_copy(out=down_s_row[0:1, :], in_=down_s_stage[:])

        channel_scales = fixed.tile([P, 16], F32)
        down_s_all = fixed.tile([P, HIDDEN], F32)

        def spread_channel_scales():
            channel_bank = banks.tile([P, BANK], F32, tag="bank")
            channel_words = channel_rows[:].bitcast(F32)
            for h in range(2):
                nc.tensor.transpose(
                    channel_bank[:, h * P : (h + 1) * P], channel_words[:, h : 2 * P - 1 + h : 2], identity[:]
                )
            nc.vector.tensor_copy(
                out=channel_scales[:].rearrange("p (r h e) -> p h r e", h=2, e=2),
                in_=channel_bank[:, 0 : 2 * P].bitcast(BF16).rearrange("p (h r e) -> p h r e", h=2, e=2)[:, :, 0:4, :],
            )

        def spread_down_s():
            down_s_bank = banks.tile([P, BANK], F32, tag="bank")
            nc.tensor.matmul(out=down_s_bank[:], lhsT=ones[:], rhs=down_s_row[:], start=True, stop=True)
            nc.scalar.copy(out=down_s_all[:], in_=down_s_bank[:])

        codes = {}
        scales = {}
        grouped_of = {}
        hidden_rows = []
        hidden_grouped = []
        hidden_codes = []
        hidden_scales = []

        def transpose(n, first=0, count=2):
            grouped = fixed.tile([P, count * K_PASS], BF16, name="grouped%d_%d" % (n, first), align_bytes=64)
            raw = unit_raw[n][:, first * K_PASS : (first + count) * K_PASS]
            k_onto_partitions(nc, banks, identity, raw, grouped[:], nc.scalar.copy)
            grouped_of[n, first] = grouped

        def quantise_tiles(n, first=0, count=2):
            unit_codes = fixed.tile([P, count * P], U32, name="codes%d_%d" % (n, first), align_bytes=64)
            unit_scales = fixed.tile([P, count * P], U8, name="scales%d_%d" % (n, first), align_bytes=64)
            quantise(nc, grouped_of[n, first], unit_codes, unit_scales)
            for i in range(count):
                cols = slice(i * P, (i + 1) * P)
                codes[n, first + i] = unit_codes[:, cols].bitcast(FP8X4)
                scales[n, first + i] = unit_scales[:, cols]

        def multiply(n, bank):
            for e in range(2):
                nc.tensor.matmul_mx(
                    out=bank[:, e * P : (e + 1) * P],
                    lhsT=codes[n, e],
                    lhsT_scale=scales[n, e],
                    rhs=x_codes[:].bitcast(FP8X4),
                    rhs_scale=x_scales[:],
                    start=True,
                    stop=True,
                )

        def hidden_tiles(m):
            g_bank = banks.tile([P, BANK], F32, tag="bank")
            u_bank = banks.tile([P, BANK], F32, tag="bank")
            multiply(2 * m, g_bank)
            multiply(2 * m + 1, u_bank)
            if m % 2 == 0:
                hidden_rows.append(fixed.tile([P, PACK * P], BF16, name="hidden_rows%d" % (m // 2)))
            silu_g = work.tile([P, 2 * P], F32)
            for e in range(2):
                cols = slice(e * P, (e + 1) * P)
                channel = 2 * m + e
                t = channel % PACK
                nc.scalar.activation(
                    out=silu_g[:, cols],
                    in_=g_bank[:, cols],
                    func=SILU,
                    scale=channel_scales[:, channel : channel + 1],
                )
                nc.vector.scalar_tensor_tensor(
                    out=hidden_rows[m // 2][:, t * P : (t + 1) * P],
                    in0=u_bank[:, cols],
                    scalar=channel_scales[:, 8 + channel : 9 + channel],
                    in1=silu_g[:, cols],
                    op0=MULT,
                    op1=MULT,
                )

        def regroup_hidden(c):
            hidden_grouped.append(fixed.tile([P, P * PACK], BF16, name="hidden_grouped%d" % c, align_bytes=64))
            nc.vector.tensor_copy(
                out=hidden_grouped[c][:].rearrange("p (w t) -> p w t", t=PACK),
                in_=hidden_rows[c][:].rearrange("p (t w) -> p w t", t=PACK),
            )

        def quantise_hidden(c):
            hidden_codes.append(fixed.tile([P, P], U32, name="hidden_codes%d" % c, align_bytes=64))
            hidden_scales.append(fixed.tile([P, P], U8, name="hidden_scales%d" % c, align_bytes=64))
            quantise(nc, hidden_grouped[c], hidden_codes[c], hidden_scales[c])

        for n in range(6):
            transpose(n)
            if n == 1:
                spread_channel_scales()
            quantise_tiles(n)
        hidden_tiles(0)
        for n in (6, 7):
            transpose(n)
            quantise_tiles(n)
        transpose(8)
        hidden_tiles(1)
        quantise_tiles(8)
        regroup_hidden(0)
        transpose(9)
        hidden_tiles(2)
        hidden_tiles(3)
        quantise_hidden(0)
        regroup_hidden(1)
        quantise_tiles(9)
        quantise_hidden(1)
        transpose(10)
        quantise_tiles(10)
        for c in range(INNER_PASSES):
            transpose(11, c, 1)
        spread_down_s()
        for c in range(INNER_PASSES):
            quantise_tiles(11, c, 1)

        for blocks in ((0, 1), (2,), (3,)):
            out_bank = banks.tile([P, BANK], F32, tag="bank")
            width = len(blocks) * P
            for b, j in enumerate(blocks):
                for c in range(INNER_PASSES):
                    nc.tensor.matmul_mx(
                        out=out_bank[:, b * P : (b + 1) * P],
                        lhsT=hidden_codes[c][:].bitcast(FP8X4),
                        lhsT_scale=hidden_scales[c][:],
                        rhs=codes[first_down + j, c],
                        rhs_scale=scales[first_down + j, c],
                        start=(c == 0),
                        stop=(c == INNER_PASSES - 1),
                    )
            channels = slice(blocks[0] * P, blocks[0] * P + width)
            result = work.tile([P, 2 * P], F32, bufs=3)
            nc.vector.tensor_tensor(
                out=result[:, 0:width], in0=out_bank[:, 0:width], in1=down_s_all[:, channels], op=MULT
            )
            nc.sync.dma_start(out=out_rows[:, channels], in_=result[:, 0:width])
